import numpy as np
import ml_dtypes


def mxq(x, axis, fmt="e4m3"):
    dtype, down = {"e4m3": (ml_dtypes.float8_e4m3fn, 7), "e5m2": (ml_dtypes.float8_e5m2, 14)}[fmt]
    v = np.moveaxis(np.asarray(x, np.float32).astype(ml_dtypes.bfloat16).astype(np.float64), axis, -1)
    blocks = v.reshape(v.shape[:-1] + (-1, 32))
    amax = np.abs(blocks).max(-1, keepdims=True)
    byte = np.maximum(np.where(amax > 0, np.frexp(amax)[1] - 1 + 127, 0) - down, 1)
    scale = np.exp2(byte - 127.0)
    codes = (blocks / scale).astype(np.float32).astype(dtype).astype(np.float64)
    return np.moveaxis((codes * scale).reshape(v.shape), -1, axis)


WIDE = False


def mx_kscale(k):
    if not WIDE:
        return np.ones(k)
    levels = np.array([10, -10, 5, -5, 0])
    a = np.random.permutation(np.resize(levels, k // 512 * 4)).reshape(k // 512, 4)
    idx = np.arange(k)
    return np.exp2(a[idx // 512, idx % 128 // 32])


BF16 = ml_dtypes.bfloat16


def bf(x):
    return np.asarray(x, np.float32).astype(BF16)


def f64(x):
    return np.asarray(x).astype(np.float64)


B, H, T, D = 1, 16, 512, 128
QS = 0.7 / D ** 0.25
VS = 4.0 / np.sqrt(T)


def setup_inputs():
    u = mx_kscale(T)
    return {"q_rot": bf(np.random.standard_normal((B, H, T, D)) * QS * u[:, None]),
            "v": bf(np.random.standard_normal((B, H, T, D)) * VS / (u * u.max())[:, None])}


def reference(q_rot, v):
    scores = f64(q_rot) @ f64(q_rot).transpose(0, 1, 3, 2)
    return mxq(scores, 3, "e4m3") @ mxq(f64(v), 2, "e4m3")

@@ -1,0 +1,146 @@
+from contextlib import ExitStack
+
+import concourse.mybir as mybir
+from concourse.masks import make_identity
+
+BF16 = mybir.dt.bfloat16
+F32 = mybir.dt.float32
+U32 = mybir.dt.uint32
+U8 = mybir.dt.uint8
+FP8X4 = mybir.dt.float8_e4m3fn_x4
+
+P = 128
+PACK = 4
+H, T, D = 16, 512, 128
+FLOPS = 2 * 2 * H * T * T * D
+
+Q_CHUNKS = [(0, 1), (1, 1), (2, 2), (4, 4), (8, 4), (12, 4)]
+V_GROUP = 4
+
+
+def tile_linearattention_pa_kernel(tc, q_rot, v, out):
+    nc = tc.nc
+    qv = q_rot.rearrange("b h (p j) d -> p (b h) j d", j=PACK)
+    vv = v.rearrange("b h (p j) d -> p (b h) j d", j=PACK)
+    ov = out.rearrange("b h (p j) d -> p (b h) j d", j=PACK)
+
+    with ExitStack() as ctx:
+        keep = ctx.enter_context(tc.tile_pool(name="keep", bufs=1))
+        qt_pool = ctx.enter_context(tc.tile_pool(name="qtp", bufs=4))
+        g_pool = ctx.enter_context(tc.tile_pool(name="gp", bufs=3))
+        c_pool = ctx.enter_context(tc.tile_pool(name="cp", bufs=4))
+        vg_pool = ctx.enter_context(tc.tile_pool(name="vgp", bufs=2))
+        o_pool = ctx.enter_context(tc.tile_pool(name="op", bufs=4))
+        psum_t = ctx.enter_context(tc.psum_pool(name="pst", bufs=2))
+        psum_s = ctx.enter_context(tc.psum_pool(name="pss", bufs=4))
+        psum_o = ctx.enter_context(tc.psum_pool(name="pso", bufs=2))
+
+        ident = keep.tile([P, P], BF16, name="ident")
+        make_identity(nc, ident[:])
+
+        q_head = {}
+        v_tiles = {}
+
+        def load_q(h0, n):
+            qs = keep.tile([P, n, PACK, D], BF16, name="q%d" % h0)
+            nc.sync.dma_start(out=qs[:], in_=qv[:, h0:h0 + n])
+            for k in range(n):
+                q_head[h0 + k] = qs[:, k]
+
+        def load_v(grp):
+            vs_ = keep.tile([P, V_GROUP, PACK, D], BF16, name="v%d" % grp)
+            nc.sync.dma_start(out=vs_[:], in_=vv[:, grp * V_GROUP:(grp + 1) * V_GROUP])
+            v_tiles[grp] = vs_
+
+        load_q(0, 1)
+        load_q(1, 1)
+        load_v(0)
+        load_q(2, 2)
+        load_q(4, 4)
+        load_v(1)
+        load_q(8, 4)
+        load_v(2)
+        load_q(12, 4)
+        load_v(3)
+
+        v_codes = keep.tile([P, H * D], U32, name="v_codes", align_bytes=64)
+        v_scales = keep.tile([P, H * D], U8, name="v_scales", align_bytes=64)
+
+        qts = {}
+        gs = {}
+        codes = {}
+
+        def transposes(h):
+            pt = psum_t.tile([P, PACK, P], BF16, name="pt")
+            for j in range(PACK):
+                nc.tensor.transpose(pt[:, j, :], q_head[h][:, j, :], ident[:])
+            qt = qt_pool.tile([P, PACK, P], BF16, name="qt")
+            nc.vector.tensor_copy(out=qt[:], in_=pt[:])
+            qts[h] = qt
+
+        def v_group(grp):
+            vg = vg_pool.tile([P, V_GROUP, D, PACK], BF16, name="vg", align_bytes=64)
+            nc.vector.tensor_copy(
+                out=vg[:].rearrange("p h (c i) j -> p h c j i", i=4),
+                in_=v_tiles[grp][:].rearrange("p h j (c i) -> p h c j i", i=4),
+            )
+            cols = slice(grp * V_GROUP * D, (grp + 1) * V_GROUP * D)
+            nc.vector.quantize_mx(
+                out=v_codes[:, cols].bitcast(FP8X4),
+                scales=v_scales[:, cols],
+                in_=vg[:].rearrange("p h d j -> p (h d j)"),
+            )
+
+        def scores(h):
+            qt = qts[h]
+            g = g_pool.tile([P, PACK, P, PACK], BF16, name="g", align_bytes=64)
+            for tb in range(PACK):
+                ps = psum_s.tile([P, PACK, P], F32, name="ps")
+                for j in range(PACK):
+                    nc.tensor.matmul(ps[:, j, :], lhsT=qt[:, j, :], rhs=qt[:, tb, :], start=True, stop=True)
+                nc.scalar.copy(out=g[:, tb, :, :], in_=ps[:].rearrange("p j c -> p c j"))
+            gs[h] = g
+
+        def quantise(h):
+            sc = c_pool.tile([P, T], U32, name="sc", align_bytes=64)
+            ss = c_pool.tile([P, T], U8, name="ss", align_bytes=64)
+            nc.vector.quantize_mx(
+                out=sc[:].bitcast(FP8X4),
+                scales=ss[:],
+                in_=gs[h][:].rearrange("p b c j -> p (b c j)"),
+            )
+            codes[h] = (sc, ss)
+
+        def product(h):
+            sc, ss = codes[h]
+            po = psum_o.tile([P, PACK, D], F32, name="po")
+            vcols = slice(h * D, (h + 1) * D)
+            for tb in range(PACK):
+                cols = slice(tb * P, (tb + 1) * P)
+                nc.tensor.matmul_mx(
+                    out=po[:, tb, :],
+                    lhsT=sc[:, cols].bitcast(FP8X4),
+                    lhsT_scale=ss[:, cols],
+                    rhs=v_codes[:, vcols].bitcast(FP8X4),
+                    rhs_scale=v_scales[:, vcols],
+                    start=True,
+                    stop=True,
+                )
+            o_sb = o_pool.tile([P, PACK, D], F32, name="o_sb")
+            nc.vector.tensor_copy(out=o_sb[:], in_=po[:])
+            nc.sync.dma_start(out=ov[:, h], in_=o_sb[:])
+
+        transposes(0)
+        transposes(1)
+        v_group(0)
+        for i in range(H + 2):
+            if i < H:
+                scores(i)
+            if i + 2 < H:
+                transposes(i + 2)
+            if 0 <= i - 1 < H:
+                quantise(i - 1)
+            if i % V_GROUP == 1 and i // V_GROUP + 1 < H // V_GROUP:
+                v_group(i // V_GROUP + 1)
+            if i - 2 >= 0:
+                product(i - 2)

@@ -13,9 +13,10 @@ P = 128
 PACK = 4
 H, T, D = 16, 512, 128
 FLOPS = 2 * 2 * H * T * T * D
-
-Q_CHUNKS = [(0, 1), (1, 1), (2, 2), (4, 4), (8, 4), (12, 4)]
 V_GROUP = 4
+
+VECTOR_BANKS = ((2, 1), (5, 1), (8, 1), (11, 1), (12, 2), (12, 3), (14, 1))
+V_AT = {0: 0, 1: 1, 6: 2, 10: 3}
 
 
 def tile_linearattention_pa_kernel(tc, q_rot, v, out):
@@ -31,9 +32,10 @@ def tile_linearattention_pa_kernel(tc, q_rot, v, out):
         c_pool = ctx.enter_context(tc.tile_pool(name="cp", bufs=4))
         vg_pool = ctx.enter_context(tc.tile_pool(name="vgp", bufs=2))
         o_pool = ctx.enter_context(tc.tile_pool(name="op", bufs=4))
-        psum_t = ctx.enter_context(tc.psum_pool(name="pst", bufs=2))
-        psum_s = ctx.enter_context(tc.psum_pool(name="pss", bufs=4))
+        psum_t = ctx.enter_context(tc.psum_pool(name="pst", bufs=1))
+        psum_s = ctx.enter_context(tc.psum_pool(name="pss", bufs=5))
         psum_o = ctx.enter_context(tc.psum_pool(name="pso", bufs=2))
+        ctx.enter_context(tc.manual_schedule())
 
         ident = keep.tile([P, P], BF16, name="ident")
         make_identity(nc, ident[:])
@@ -66,59 +68,78 @@ def tile_linearattention_pa_kernel(tc, q_rot, v, out):
         v_codes = keep.tile([P, H * D], U32, name="v_codes", align_bytes=64)
         v_scales = keep.tile([P, H * D], U8, name="v_scales", align_bytes=64)
 
+        pts = {}
         qts = {}
+        banks = {}
         gs = {}
         codes = {}
+        vgs = {}
+        pos = {}
 
         def transposes(h):
             pt = psum_t.tile([P, PACK, P], BF16, name="pt")
             for j in range(PACK):
                 nc.tensor.transpose(pt[:, j, :], q_head[h][:, j, :], ident[:])
+            pts[h] = pt
+
+        def qt_out(h):
             qt = qt_pool.tile([P, PACK, P], BF16, name="qt")
-            nc.vector.tensor_copy(out=qt[:], in_=pt[:])
+            nc.vector.tensor_copy(out=qt[:], in_=pts[h][:])
             qts[h] = qt
 
-        def v_group(grp):
+        def v_regroup(grp):
             vg = vg_pool.tile([P, V_GROUP, D, PACK], BF16, name="vg", align_bytes=64)
             nc.vector.tensor_copy(
                 out=vg[:].rearrange("p h (c i) j -> p h c j i", i=4),
                 in_=v_tiles[grp][:].rearrange("p h j (c i) -> p h c j i", i=4),
             )
+            vgs[grp] = vg
+
+        def v_quantise(grp):
             cols = slice(grp * V_GROUP * D, (grp + 1) * V_GROUP * D)
             nc.vector.quantize_mx(
                 out=v_codes[:, cols].bitcast(FP8X4),
                 scales=v_scales[:, cols],
-                in_=vg[:].rearrange("p h d j -> p (h d j)"),
+                in_=vgs[grp][:].rearrange("p h d j -> p (h d j)"),
             )
 
-        def scores(h):
+        def scores(h, tb):
             qt = qts[h]
-            g = g_pool.tile([P, PACK, P, PACK], BF16, name="g", align_bytes=64)
-            for tb in range(PACK):
-                ps = psum_s.tile([P, PACK, P], F32, name="ps")
-                for j in range(PACK):
-                    nc.tensor.matmul(ps[:, j, :], lhsT=qt[:, j, :], rhs=qt[:, tb, :], start=True, stop=True)
-                nc.scalar.copy(out=g[:, tb, :, :], in_=ps[:].rearrange("p j c -> p c j"))
-            gs[h] = g
+            ps = psum_s.tile([P, PACK, P], F32, name="ps")
+            for j in range(PACK):
+                nc.tensor.matmul(ps[:, j, :], lhsT=qt[:, j, :], rhs=qt[:, tb, :], start=True, stop=True)
+            banks[(h, tb)] = ps
 
-        def quantise(h):
-            sc = c_pool.tile([P, T], U32, name="sc", align_bytes=64)
-            ss = c_pool.tile([P, T], U8, name="ss", align_bytes=64)
+        def scores_out(h, tb):
+            if tb == 0:
+                gs[h] = g_pool.tile([P, PACK, P, PACK], BF16, name="g", align_bytes=64)
+            src = banks[(h, tb)][:].rearrange("p j c -> p c j")
+            if (h, tb) in VECTOR_BANKS:
+                nc.vector.tensor_copy(out=gs[h][:, tb, :, :], in_=src)
+            else:
+                nc.scalar.copy(out=gs[h][:, tb, :, :], in_=src)
+
+        def quantise(h, tb0, n):
+            if tb0 == 0:
+                sc_new = c_pool.tile([P, T], U32, name="sc", align_bytes=64)
+                ss_new = c_pool.tile([P, T], U8, name="ss", align_bytes=64)
+                codes[h] = (sc_new, ss_new)
+            sc, ss = codes[h]
+            cols = slice(tb0 * P, (tb0 + n) * P)
             nc.vector.quantize_mx(
-                out=sc[:].bitcast(FP8X4),
-                scales=ss[:],
-                in_=gs[h][:].rearrange("p b c j -> p (b c j)"),
+                out=sc[:, cols].bitcast(FP8X4),
+                scales=ss[:, cols],
+                in_=gs[h][:, tb0:tb0 + n].rearrange("p b c j -> p (b c j)"),
             )
-            codes[h] = (sc, ss)
 
-        def product(h):
+        def product(h, tb0, n):
             sc, ss = codes[h]
             po = psum_o.tile([P, PACK, D], F32, name="po")
             vcols = slice(h * D, (h + 1) * D)
-            for tb in range(PACK):
-                cols = slice(tb * P, (tb + 1) * P)
+            for k in range(n):
+                cols = slice((tb0 + k) * P, (tb0 + k + 1) * P)
                 nc.tensor.matmul_mx(
-                    out=po[:, tb, :],
+                    out=po[:, k, :],
                     lhsT=sc[:, cols].bitcast(FP8X4),
                     lhsT_scale=ss[:, cols],
                     rhs=v_codes[:, vcols].bitcast(FP8X4),
@@ -126,21 +147,50 @@ def tile_linearattention_pa_kernel(tc, q_rot, v, out):
                     start=True,
                     stop=True,
                 )
+            pos[(h, tb0)] = po
+
+        def product_out(h, tb0, n, on_scalar):
             o_sb = o_pool.tile([P, PACK, D], F32, name="o_sb")
-            nc.vector.tensor_copy(out=o_sb[:], in_=po[:])
-            nc.sync.dma_start(out=ov[:, h], in_=o_sb[:])
+            if on_scalar:
+                nc.scalar.copy(out=o_sb[:, 0:n, :], in_=pos[(h, tb0)][:, 0:n, :])
+            else:
+                nc.vector.tensor_copy(out=o_sb[:, 0:n, :], in_=pos[(h, tb0)][:, 0:n, :])
+            nc.sync.dma_start(out=ov[:, h, tb0:tb0 + n], in_=o_sb[:, 0:n, :])
 
         transposes(0)
+        qt_out(0)
         transposes(1)
-        v_group(0)
-        for i in range(H + 2):
-            if i < H:
-                scores(i)
+        qt_out(1)
+        for i in range(H):
+            scores(i, 0)
+            scores(i, 1)
             if i + 2 < H:
                 transposes(i + 2)
-            if 0 <= i - 1 < H:
-                quantise(i - 1)
-            if i % V_GROUP == 1 and i // V_GROUP + 1 < H // V_GROUP:
-                v_group(i // V_GROUP + 1)
-            if i - 2 >= 0:
-                product(i - 2)
+            scores(i, 2)
+            scores(i, 3)
+            if i >= 2:
+                product(i - 2, 0, PACK)
+            scores_out(i, 0)
+            if i >= 3:
+                product_out(i - 3, 0, PACK, False)
+            scores_out(i, 1)
+            if i in V_AT:
+                v_regroup(V_AT[i])
+            if i == H - 1:
+                quantise(i, 0, 2)
+            if i + 2 < H:
+                qt_out(i + 2)
+            scores_out(i, 2)
+            if i >= 1:
+                quantise(i - 1, 0, PACK)
+            scores_out(i, 3)
+            if i in V_AT:
+                v_quantise(V_AT[i])
+        product(H - 2, 0, PACK)
+        quantise(H - 1, 2, 2)
+        product_out(H - 3, 0, PACK, True)
+        product(H - 1, 0, 2)
+        product_out(H - 2, 0, PACK, False)
+        product(H - 1, 2, 2)
+        product_out(H - 1, 0, 2, True)
+        product_out(H - 1, 2, 2, False)

@@ -15,8 +15,7 @@ H, T, D = 16, 512, 128
 FLOPS = 2 * 2 * H * T * T * D
 V_GROUP = 4
 
-VECTOR_BANKS = ((2, 1), (5, 1), (8, 1), (11, 1), (12, 2), (12, 3), (14, 1))
-V_AT = {0: 0, 1: 1, 6: 2, 10: 3}
+VECTOR_BANKS = ((0, 0), (0, 3), (1, 2), (2, 1), (3, 1), (5, 1), (8, 1), (8, 2), (11, 1), (11, 3), (14, 1))
 
 
 def tile_linearattention_pa_kernel(tc, q_rot, v, out):
@@ -87,20 +86,24 @@ def tile_linearattention_pa_kernel(tc, q_rot, v, out):
             nc.vector.tensor_copy(out=qt[:], in_=pts[h][:])
             qts[h] = qt
 
-        def v_regroup(grp):
-            vg = vg_pool.tile([P, V_GROUP, D, PACK], BF16, name="vg", align_bytes=64)
-            nc.vector.tensor_copy(
-                out=vg[:].rearrange("p h (c i) j -> p h c j i", i=4),
-                in_=v_tiles[grp][:].rearrange("p h j (c i) -> p h c j i", i=4),
+        def v_regroup(h):
+            vg = vg_pool.tile([P, D, PACK], BF16, name="vg", align_bytes=64)
+            nc.gpsimd.tensor_scalar(
+                out=vg[:],
+                in0=v_tiles[h // V_GROUP][:, h % V_GROUP].rearrange("p j d -> p d j"),
+                scalar1=1.0,
+                scalar2=0.0,
+                op0=mybir.AluOpType.mult,
+                op1=mybir.AluOpType.add,
             )
-            vgs[grp] = vg
+            vgs[h] = vg
 
-        def v_quantise(grp):
-            cols = slice(grp * V_GROUP * D, (grp + 1) * V_GROUP * D)
+        def v_quantise(h):
+            cols = slice(h * D, (h + 1) * D)
             nc.vector.quantize_mx(
                 out=v_codes[:, cols].bitcast(FP8X4),
                 scales=v_scales[:, cols],
-                in_=vgs[grp][:].rearrange("p h d j -> p (h d j)"),
+                in_=vgs[h][:].rearrange("p d j -> p (d j)"),
             )
 
         def scores(h, tb):
@@ -161,6 +164,8 @@ def tile_linearattention_pa_kernel(tc, q_rot, v, out):
         qt_out(0)
         transposes(1)
         qt_out(1)
+        v_regroup(0)
+        v_regroup(1)
         for i in range(H):
             scores(i, 0)
             scores(i, 1)
@@ -174,8 +179,6 @@ def tile_linearattention_pa_kernel(tc, q_rot, v, out):
             if i >= 3:
                 product_out(i - 3, 0, PACK, False)
             scores_out(i, 1)
-            if i in V_AT:
-                v_regroup(V_AT[i])
             if i == H - 1:
                 quantise(i, 0, 2)
             if i + 2 < H:
@@ -183,9 +186,10 @@ def tile_linearattention_pa_kernel(tc, q_rot, v, out):
             scores_out(i, 2)
             if i >= 1:
                 quantise(i - 1, 0, PACK)
+            v_quantise(i)
+            if i + 2 < H:
+                v_regroup(i + 2)
             scores_out(i, 3)
-            if i in V_AT:
-                v_quantise(V_AT[i])
         product(H - 2, 0, PACK)
         quantise(H - 1, 2, 2)
         product_out(H - 3, 0, PACK, True)

@@ -15,7 +15,8 @@ H, T, D = 16, 512, 128
 FLOPS = 2 * 2 * H * T * T * D
 V_GROUP = 4
 
-VECTOR_BANKS = ((0, 0), (0, 3), (1, 2), (2, 1), (3, 1), (5, 1), (8, 1), (8, 2), (11, 1), (11, 3), (14, 1))
+HALF = 2
+VECTOR_UNITS = ((1, 0), (2, 1), (6, 1), (10, 1), (14, 1))
 
 
 def tile_linearattention_pa_kernel(tc, q_rot, v, out):
@@ -31,8 +32,8 @@ def tile_linearattention_pa_kernel(tc, q_rot, v, out):
         c_pool = ctx.enter_context(tc.tile_pool(name="cp", bufs=4))
         vg_pool = ctx.enter_context(tc.tile_pool(name="vgp", bufs=2))
         o_pool = ctx.enter_context(tc.tile_pool(name="op", bufs=4))
-        psum_t = ctx.enter_context(tc.psum_pool(name="pst", bufs=1))
-        psum_s = ctx.enter_context(tc.psum_pool(name="pss", bufs=5))
+        psum_t = ctx.enter_context(tc.psum_pool(name="pst", bufs=2))
+        psum_s = ctx.enter_context(tc.psum_pool(name="pss", bufs=4))
         psum_o = ctx.enter_context(tc.psum_pool(name="pso", bufs=2))
         ctx.enter_context(tc.manual_schedule())
 
@@ -106,21 +107,23 @@ def tile_linearattention_pa_kernel(tc, q_rot, v, out):
                 in_=vgs[h][:].rearrange("p d j -> p (d j)"),
             )
 
-        def scores(h, tb):
+        def scores(h, u):
             qt = qts[h]
-            ps = psum_s.tile([P, PACK, P], F32, name="ps")
+            ps = psum_s.tile([P, PACK, HALF * P], BF16, name="ps")
+            moving = qt[:, HALF * u:HALF * (u + 1), :].rearrange("p b c -> p (b c)")
             for j in range(PACK):
-                nc.tensor.matmul(ps[:, j, :], lhsT=qt[:, j, :], rhs=qt[:, tb, :], start=True, stop=True)
-            banks[(h, tb)] = ps
+                nc.tensor.matmul(ps[:, j, :], lhsT=qt[:, j, :], rhs=moving, start=True, stop=True)
+            banks[(h, u)] = ps
 
-        def scores_out(h, tb):
-            if tb == 0:
+        def scores_out(h, u):
+            if u == 0:
                 gs[h] = g_pool.tile([P, PACK, P, PACK], BF16, name="g", align_bytes=64)
-            src = banks[(h, tb)][:].rearrange("p j c -> p c j")
-            if (h, tb) in VECTOR_BANKS:
-                nc.vector.tensor_copy(out=gs[h][:, tb, :, :], in_=src)
+            src = banks[(h, u)][:].rearrange("p j c -> p c j")
+            dst = gs[h][:, HALF * u:HALF * (u + 1)].rearrange("p b c j -> p (b c) j")
+            if (h, u) in VECTOR_UNITS:
+                nc.vector.tensor_copy(out=dst, in_=src)
             else:
-                nc.scalar.copy(out=gs[h][:, tb, :, :], in_=src)
+                nc.scalar.copy(out=dst, in_=src)
 
         def quantise(h, tb0, n):
             if tb0 == 0:
@@ -168,28 +171,24 @@ def tile_linearattention_pa_kernel(tc, q_rot, v, out):
         v_regroup(1)
         for i in range(H):
             scores(i, 0)
-            scores(i, 1)
             if i + 2 < H:
                 transposes(i + 2)
-            scores(i, 2)
-            scores(i, 3)
+            scores(i, 1)
             if i >= 2:
                 product(i - 2, 0, PACK)
             scores_out(i, 0)
             if i >= 3:
                 product_out(i - 3, 0, PACK, False)
-            scores_out(i, 1)
             if i == H - 1:
                 quantise(i, 0, 2)
             if i + 2 < H:
                 qt_out(i + 2)
-            scores_out(i, 2)
             if i >= 1:
                 quantise(i - 1, 0, PACK)
             v_quantise(i)
             if i + 2 < H:
                 v_regroup(i + 2)
-            scores_out(i, 3)
+            scores_out(i, 1)
         product(H - 2, 0, PACK)
         quantise(H - 1, 2, 2)
         product_out(H - 3, 0, PACK, True)

@@ -13,10 +13,10 @@ P = 128
 PACK = 4
 H, T, D = 16, 512, 128
 FLOPS = 2 * 2 * H * T * T * D
-V_GROUP = 4
 
-HALF = 2
-VECTOR_UNITS = ((1, 0), (2, 1), (6, 1), (10, 1), (14, 1))
+PAIR = 2
+VECTOR_BANKS = tuple((i, tb) for i in range(0, 14, 2) for tb in (2, 3)) + ((14, 0),)
+SCALAR_PRODUCTS = (1, 3, 5, 7)
 
 
 def tile_linearattention_pa_kernel(tc, q_rot, v, out):
@@ -30,10 +30,10 @@ def tile_linearattention_pa_kernel(tc, q_rot, v, out):
         qt_pool = ctx.enter_context(tc.tile_pool(name="qtp", bufs=4))
         g_pool = ctx.enter_context(tc.tile_pool(name="gp", bufs=3))
         c_pool = ctx.enter_context(tc.tile_pool(name="cp", bufs=4))
-        vg_pool = ctx.enter_context(tc.tile_pool(name="vgp", bufs=2))
+        vg_pool = ctx.enter_context(tc.tile_pool(name="vgp", bufs=1))
         o_pool = ctx.enter_context(tc.tile_pool(name="op", bufs=4))
-        psum_t = ctx.enter_context(tc.psum_pool(name="pst", bufs=2))
-        psum_s = ctx.enter_context(tc.psum_pool(name="pss", bufs=4))
+        psum_t = ctx.enter_context(tc.psum_pool(name="pst", bufs=1))
+        psum_s = ctx.enter_context(tc.psum_pool(name="pss", bufs=5))
         psum_o = ctx.enter_context(tc.psum_pool(name="pso", bufs=2))
         ctx.enter_context(tc.manual_schedule())
 
@@ -41,7 +41,7 @@ def tile_linearattention_pa_kernel(tc, q_rot, v, out):
         make_identity(nc, ident[:])
 
         q_head = {}
-        v_tiles = {}
+        v_pair = {}
 
         def load_q(h0, n):
             qs = keep.tile([P, n, PACK, D], BF16, name="q%d" % h0)
@@ -49,21 +49,25 @@ def tile_linearattention_pa_kernel(tc, q_rot, v, out):
             for k in range(n):
                 q_head[h0 + k] = qs[:, k]
 
-        def load_v(grp):
-            vs_ = keep.tile([P, V_GROUP, PACK, D], BF16, name="v%d" % grp)
-            nc.sync.dma_start(out=vs_[:], in_=vv[:, grp * V_GROUP:(grp + 1) * V_GROUP])
-            v_tiles[grp] = vs_
+        def load_v(h0):
+            vs_ = keep.tile([P, PAIR, PACK, D], BF16, name="v%d" % h0)
+            nc.sync.dma_start(out=vs_[:], in_=vv[:, h0:h0 + PAIR])
+            v_pair[h0] = vs_
 
         load_q(0, 1)
         load_q(1, 1)
         load_v(0)
         load_q(2, 2)
-        load_q(4, 4)
-        load_v(1)
-        load_q(8, 4)
         load_v(2)
+        load_q(4, 4)
+        load_v(4)
+        load_v(6)
+        load_q(8, 4)
+        load_v(8)
+        load_v(10)
         load_q(12, 4)
-        load_v(3)
+        load_v(12)
+        load_v(14)
 
         v_codes = keep.tile([P, H * D], U32, name="v_codes", align_bytes=64)
         v_scales = keep.tile([P, H * D], U8, name="v_scales", align_bytes=64)
@@ -87,43 +91,41 @@ def tile_linearattention_pa_kernel(tc, q_rot, v, out):
             nc.vector.tensor_copy(out=qt[:], in_=pts[h][:])
             qts[h] = qt
 
-        def v_regroup(h):
-            vg = vg_pool.tile([P, D, PACK], BF16, name="vg", align_bytes=64)
+        def v_regroup(h0):
+            vg = vg_pool.tile([P, PAIR, D, PACK], BF16, name="vg", align_bytes=64)
             nc.gpsimd.tensor_scalar(
                 out=vg[:],
-                in0=v_tiles[h // V_GROUP][:, h % V_GROUP].rearrange("p j d -> p d j"),
+                in0=v_pair[h0][:].rearrange("p h j d -> p h d j"),
                 scalar1=1.0,
                 scalar2=0.0,
                 op0=mybir.AluOpType.mult,
                 op1=mybir.AluOpType.add,
             )
-            vgs[h] = vg
+            vgs[h0] = vg
 
-        def v_quantise(h):
-            cols = slice(h * D, (h + 1) * D)
+        def v_quantise(h0):
+            cols = slice(h0 * D, (h0 + PAIR) * D)
             nc.vector.quantize_mx(
                 out=v_codes[:, cols].bitcast(FP8X4),
                 scales=v_scales[:, cols],
-                in_=vgs[h][:].rearrange("p d j -> p (d j)"),
+                in_=vgs[h0][:].rearrange("p h d j -> p (h d j)"),
             )
 
-        def scores(h, u):
+        def scores(h, tb):
             qt = qts[h]
-            ps = psum_s.tile([P, PACK, HALF * P], BF16, name="ps")
-            moving = qt[:, HALF * u:HALF * (u + 1), :].rearrange("p b c -> p (b c)")
+            ps = psum_s.tile([P, PACK, P], F32, name="ps")
             for j in range(PACK):
-                nc.tensor.matmul(ps[:, j, :], lhsT=qt[:, j, :], rhs=moving, start=True, stop=True)
-            banks[(h, u)] = ps
+                nc.tensor.matmul(ps[:, j, :], lhsT=qt[:, j, :], rhs=qt[:, tb, :], start=True, stop=True)
+            banks[(h, tb)] = ps
 
-        def scores_out(h, u):
-            if u == 0:
+        def scores_out(h, tb):
+            if tb == 0:
                 gs[h] = g_pool.tile([P, PACK, P, PACK], BF16, name="g", align_bytes=64)
-            src = banks[(h, u)][:].rearrange("p j c -> p c j")
-            dst = gs[h][:, HALF * u:HALF * (u + 1)].rearrange("p b c j -> p (b c) j")
-            if (h, u) in VECTOR_UNITS:
-                nc.vector.tensor_copy(out=dst, in_=src)
+            src = banks[(h, tb)][:].rearrange("p j c -> p c j")
+            if (h, tb) in VECTOR_BANKS:
+                nc.vector.tensor_copy(out=gs[h][:, tb, :, :], in_=src)
             else:
-                nc.scalar.copy(out=dst, in_=src)
+                nc.scalar.copy(out=gs[h][:, tb, :, :], in_=src)
 
         def quantise(h, tb0, n):
             if tb0 == 0:
@@ -138,9 +140,12 @@ def tile_linearattention_pa_kernel(tc, q_rot, v, out):
                 in_=gs[h][:, tb0:tb0 + n].rearrange("p b c j -> p (b c j)"),
             )
 
-        def product(h, tb0, n):
+        def product(h, tb0, n, in_score_bank):
             sc, ss = codes[h]
-            po = psum_o.tile([P, PACK, D], F32, name="po")
+            if in_score_bank:
+                po = psum_s.tile([P, PACK, D], F32, name="ps")
+            else:
+                po = psum_o.tile([P, PACK, D], F32, name="po")
             vcols = slice(h * D, (h + 1) * D)
             for k in range(n):
                 cols = slice((tb0 + k) * P, (tb0 + k + 1) * P)
@@ -165,35 +170,39 @@ def tile_linearattention_pa_kernel(tc, q_rot, v, out):
 
         transposes(0)
         qt_out(0)
+        v_regroup(0)
         transposes(1)
         qt_out(1)
-        v_regroup(0)
-        v_regroup(1)
         for i in range(H):
             scores(i, 0)
+            scores(i, 1)
             if i + 2 < H:
                 transposes(i + 2)
-            scores(i, 1)
+            scores(i, 2)
+            scores(i, 3)
             if i >= 2:
-                product(i - 2, 0, PACK)
+                product(i - 2, 0, PACK, False)
             scores_out(i, 0)
             if i >= 3:
-                product_out(i - 3, 0, PACK, False)
+                product_out(i - 3, 0, PACK, (i - 3) in SCALAR_PRODUCTS)
+            scores_out(i, 1)
             if i == H - 1:
                 quantise(i, 0, 2)
             if i + 2 < H:
                 qt_out(i + 2)
             if i >= 1:
                 quantise(i - 1, 0, PACK)
-            v_quantise(i)
-            if i + 2 < H:
-                v_regroup(i + 2)
-            scores_out(i, 1)
-        product(H - 2, 0, PACK)
+            if i % PAIR == 0:
+                v_quantise(i)
+                if i + PAIR < H:
+                    v_regroup(i + PAIR)
+            scores_out(i, 2)
+            scores_out(i, 3)
+        product(H - 2, 0, PACK, False)
+        product(H - 1, 0, 2, True)
         quantise(H - 1, 2, 2)
+        product(H - 1, 2, 2, True)
         product_out(H - 3, 0, PACK, True)
-        product(H - 1, 0, 2)
-        product_out(H - 2, 0, PACK, False)
-        product(H - 1, 2, 2)
-        product_out(H - 1, 0, 2, True)
+        product_out(H - 1, 0, 2, False)
+        product_out(H - 2, 0, PACK, True)
         product_out(H - 1, 2, 2, False)

@@ -15,7 +15,8 @@ H, T, D = 16, 512, 128
 FLOPS = 2 * 2 * H * T * T * D
 
 PAIR = 2
-VECTOR_BANKS = tuple((i, tb) for i in range(0, 14, 2) for tb in (2, 3)) + ((14, 0),)
+HALF = 2
+VECTOR_UNITS = tuple((i, 1) for i in range(0, 14, 2))
 SCALAR_PRODUCTS = (1, 3, 5, 7)
 
 
@@ -32,8 +33,8 @@ def tile_linearattention_pa_kernel(tc, q_rot, v, out):
         c_pool = ctx.enter_context(tc.tile_pool(name="cp", bufs=4))
         vg_pool = ctx.enter_context(tc.tile_pool(name="vgp", bufs=1))
         o_pool = ctx.enter_context(tc.tile_pool(name="op", bufs=4))
-        psum_t = ctx.enter_context(tc.psum_pool(name="pst", bufs=1))
-        psum_s = ctx.enter_context(tc.psum_pool(name="pss", bufs=5))
+        psum_t = ctx.enter_context(tc.psum_pool(name="pst", bufs=2))
+        psum_s = ctx.enter_context(tc.psum_pool(name="pss", bufs=4))
         psum_o = ctx.enter_context(tc.psum_pool(name="pso", bufs=2))
         ctx.enter_context(tc.manual_schedule())
 
@@ -111,21 +112,23 @@ def tile_linearattention_pa_kernel(tc, q_rot, v, out):
                 in_=vgs[h0][:].rearrange("p h d j -> p (h d j)"),
             )
 
-        def scores(h, tb):
+        def scores(h, u):
             qt = qts[h]
-            ps = psum_s.tile([P, PACK, P], F32, name="ps")
+            ps = psum_s.tile([P, PACK, HALF * P], BF16, name="ps")
+            moving = qt[:, HALF * u:HALF * (u + 1), :].rearrange("p b c -> p (b c)")
             for j in range(PACK):
-                nc.tensor.matmul(ps[:, j, :], lhsT=qt[:, j, :], rhs=qt[:, tb, :], start=True, stop=True)
-            banks[(h, tb)] = ps
+                nc.tensor.matmul(ps[:, j, :], lhsT=qt[:, j, :], rhs=moving, start=True, stop=True)
+            banks[(h, u)] = ps
 
-        def scores_out(h, tb):
-            if tb == 0:
+        def scores_out(h, u):
+            if u == 0:
                 gs[h] = g_pool.tile([P, PACK, P, PACK], BF16, name="g", align_bytes=64)
-            src = banks[(h, tb)][:].rearrange("p j c -> p c j")
-            if (h, tb) in VECTOR_BANKS:
-                nc.vector.tensor_copy(out=gs[h][:, tb, :, :], in_=src)
+            src = banks[(h, u)][:].rearrange("p j c -> p c j")
+            dst = gs[h][:, HALF * u:HALF * (u + 1)].rearrange("p b c j -> p (b c) j")
+            if (h, u) in VECTOR_UNITS:
+                nc.vector.tensor_copy(out=dst, in_=src)
             else:
-                nc.scalar.copy(out=gs[h][:, tb, :, :], in_=src)
+                nc.scalar.copy(out=dst, in_=src)
 
         def quantise(h, tb0, n):
             if tb0 == 0:
@@ -175,17 +178,14 @@ def tile_linearattention_pa_kernel(tc, q_rot, v, out):
         qt_out(1)
         for i in range(H):
             scores(i, 0)
-            scores(i, 1)
             if i + 2 < H:
                 transposes(i + 2)
-            scores(i, 2)
-            scores(i, 3)
+            scores(i, 1)
             if i >= 2:
                 product(i - 2, 0, PACK, False)
             scores_out(i, 0)
             if i >= 3:
                 product_out(i - 3, 0, PACK, (i - 3) in SCALAR_PRODUCTS)
-            scores_out(i, 1)
             if i == H - 1:
                 quantise(i, 0, 2)
             if i + 2 < H:
@@ -196,13 +196,12 @@ def tile_linearattention_pa_kernel(tc, q_rot, v, out):
                 v_quantise(i)
                 if i + PAIR < H:
                     v_regroup(i + PAIR)
-            scores_out(i, 2)
-            scores_out(i, 3)
+            scores_out(i, 1)
         product(H - 2, 0, PACK, False)
         product(H - 1, 0, 2, True)
         quantise(H - 1, 2, 2)
         product(H - 1, 2, 2, True)
         product_out(H - 3, 0, PACK, True)
-        product_out(H - 1, 0, 2, False)
         product_out(H - 2, 0, PACK, True)
+        product_out(H - 1, 0, 2, False)
         product_out(H - 1, 2, 2, False)

@@ -16,7 +16,17 @@ FLOPS = 2 * 2 * H * T * T * D
 
 PAIR = 2
 HALF = 2
-VECTOR_UNITS = tuple((i, 1) for i in range(0, 14, 2))
+SCALAR = 0
+VECTOR = 1
+
+
+def units_of(h):
+    if h == 0:
+        return ((0, 1, SCALAR), (1, 1, SCALAR), (2, 2, VECTOR))
+    if h == H - 1:
+        return ((0, 2, SCALAR), (2, 1, SCALAR), (3, 1, VECTOR))
+    return ((0, 2, SCALAR), (2, 2, VECTOR if h % 2 == 0 and h < H - 2 else SCALAR))
+
 SCALAR_PRODUCTS = (1, 3, 5, 7)
 
 
@@ -112,20 +122,20 @@ def tile_linearattention_pa_kernel(tc, q_rot, v, out):
                 in_=vgs[h0][:].rearrange("p h d j -> p (h d j)"),
             )
 
-        def scores(h, u):
+        def scores(h, tb0, n):
             qt = qts[h]
             ps = psum_s.tile([P, PACK, HALF * P], BF16, name="ps")
-            moving = qt[:, HALF * u:HALF * (u + 1), :].rearrange("p b c -> p (b c)")
+            moving = qt[:, tb0:tb0 + n, :].rearrange("p b c -> p (b c)")
             for j in range(PACK):
-                nc.tensor.matmul(ps[:, j, :], lhsT=qt[:, j, :], rhs=moving, start=True, stop=True)
-            banks[(h, u)] = ps
+                nc.tensor.matmul(ps[:, j, 0:n * P], lhsT=qt[:, j, :], rhs=moving, start=True, stop=True)
+            banks[(h, tb0)] = ps
 
-        def scores_out(h, u):
-            if u == 0:
+        def scores_out(h, tb0, n, engine):
+            if tb0 == 0:
                 gs[h] = g_pool.tile([P, PACK, P, PACK], BF16, name="g", align_bytes=64)
-            src = banks[(h, u)][:].rearrange("p j c -> p c j")
-            dst = gs[h][:, HALF * u:HALF * (u + 1)].rearrange("p b c j -> p (b c) j")
-            if (h, u) in VECTOR_UNITS:
+            src = banks[(h, tb0)][:, :, 0:n * P].rearrange("p j c -> p c j")
+            dst = gs[h][:, tb0:tb0 + n].rearrange("p b c j -> p (b c) j")
+            if engine == VECTOR:
                 nc.vector.tensor_copy(out=dst, in_=src)
             else:
                 nc.scalar.copy(out=dst, in_=src)
@@ -177,17 +187,18 @@ def tile_linearattention_pa_kernel(tc, q_rot, v, out):
         transposes(1)
         qt_out(1)
         for i in range(H):
-            scores(i, 0)
-            if i + 2 < H:
-                transposes(i + 2)
-            scores(i, 1)
+            units = units_of(i)
+            first = (len(units) + 1) // 2
+            for k, (tb0, n, engine) in enumerate(units):
+                scores(i, tb0, n)
+                if k == first - 1 and i + 2 < H:
+                    transposes(i + 2)
             if i >= 2:
                 product(i - 2, 0, PACK, False)
-            scores_out(i, 0)
+            for tb0, n, engine in units[:first]:
+                scores_out(i, tb0, n, engine)
             if i >= 3:
                 product_out(i - 3, 0, PACK, (i - 3) in SCALAR_PRODUCTS)
-            if i == H - 1:
-                quantise(i, 0, 2)
             if i + 2 < H:
                 qt_out(i + 2)
             if i >= 1:
@@ -196,12 +207,14 @@ def tile_linearattention_pa_kernel(tc, q_rot, v, out):
                 v_quantise(i)
                 if i + PAIR < H:
                     v_regroup(i + PAIR)
-            scores_out(i, 1)
+            for tb0, n, engine in units[first:]:
+                scores_out(i, tb0, n, engine)
+        quantise(H - 1, 0, 2)
         product(H - 2, 0, PACK, False)
         product(H - 1, 0, 2, True)
         quantise(H - 1, 2, 2)
         product(H - 1, 2, 2, True)
         product_out(H - 3, 0, PACK, True)
-        product_out(H - 2, 0, PACK, True)
-        product_out(H - 1, 0, 2, False)
+        product_out(H - 2, 0, PACK, False)
+        product_out(H - 1, 0, 2, True)
         product_out(H - 1, 2, 2, False)

@@ -28,6 +28,7 @@ def units_of(h):
     return ((0, 2, SCALAR), (2, 2, VECTOR if h % 2 == 0 and h < H - 2 else SCALAR))
 
 SCALAR_PRODUCTS = (1, 3, 5, 7)
+WARM_PASSES = 12
 
 
 def tile_linearattention_pa_kernel(tc, q_rot, v, out):
@@ -47,6 +48,12 @@ def tile_linearattention_pa_kernel(tc, q_rot, v, out):
         psum_s = ctx.enter_context(tc.psum_pool(name="pss", bufs=4))
         psum_o = ctx.enter_context(tc.psum_pool(name="pso", bufs=2))
         ctx.enter_context(tc.manual_schedule())
+
+        warm = keep.tile([P, P], BF16, name="warm")
+        nc.vector.memset(warm[:], 0.0)
+        warm_out = psum_o.tile([P, PACK, D], F32, name="po")
+        for k in range(WARM_PASSES):
+            nc.tensor.matmul(warm_out[:, k % PACK, :], lhsT=warm[:], rhs=warm[:], start=True, stop=True)
 
         ident = keep.tile([P, P], BF16, name="ident")
         make_identity(nc, ident[:])

@@ -39,11 +39,11 @@ def tile_linearattention_pa_kernel(tc, q_rot, v, out):
 
     with ExitStack() as ctx:
         keep = ctx.enter_context(tc.tile_pool(name="keep", bufs=1))
-        qt_pool = ctx.enter_context(tc.tile_pool(name="qtp", bufs=4))
-        g_pool = ctx.enter_context(tc.tile_pool(name="gp", bufs=3))
-        c_pool = ctx.enter_context(tc.tile_pool(name="cp", bufs=4))
+        qt_pool = ctx.enter_context(tc.tile_pool(name="qtp", bufs=16))
+        g_pool = ctx.enter_context(tc.tile_pool(name="gp", bufs=16))
+        c_pool = ctx.enter_context(tc.tile_pool(name="cp", bufs=16))
         vg_pool = ctx.enter_context(tc.tile_pool(name="vgp", bufs=1))
-        o_pool = ctx.enter_context(tc.tile_pool(name="op", bufs=4))
+        o_pool = ctx.enter_context(tc.tile_pool(name="op", bufs=16))
         psum_t = ctx.enter_context(tc.psum_pool(name="pst", bufs=2))
         psum_s = ctx.enter_context(tc.psum_pool(name="pss", bufs=4))
         psum_o = ctx.enter_context(tc.psum_pool(name="pso", bufs=2))

@@ -18,6 +18,7 @@ PAIR = 2
 HALF = 2
 SCALAR = 0
 VECTOR = 1
+WOVEN = ((4, 2), (9, 2), (15, 2), (15, 3),)
 
 
 def units_of(h):
@@ -131,16 +132,24 @@ def tile_linearattention_pa_kernel(tc, q_rot, v, out):
 
         def scores(h, tb0, n):
             qt = qts[h]
-            ps = psum_s.tile([P, PACK, HALF * P], BF16, name="ps")
             moving = qt[:, tb0:tb0 + n, :].rearrange("p b c -> p (b c)")
-            for j in range(PACK):
-                nc.tensor.matmul(ps[:, j, 0:n * P], lhsT=qt[:, j, :], rhs=moving, start=True, stop=True)
-            banks[(h, tb0)] = ps
+            if (h, tb0) in WOVEN:
+                ps = psum_s.tile([P, HALF * P, PACK], BF16, name="ps")
+                twice = moving.unsqueeze(2).to_broadcast([P, n * P, 2])
+                for j in (0, 2):
+                    nc.tensor.matmul(ps[:, 0:n * P, j:j + 2], lhsT=qt[:, j + 1, :], rhs=twice, start=True, stop=True)
+                    nc.tensor.matmul(ps[:, 0:n * P, j], lhsT=qt[:, j, :], rhs=moving, start=True, stop=True)
+                banks[(h, tb0)] = ps[:, 0:n * P, :]
+            else:
+                ps = psum_s.tile([P, PACK, HALF * P], BF16, name="ps")
+                for j in range(PACK):
+                    nc.tensor.matmul(ps[:, j, 0:n * P], lhsT=qt[:, j, :], rhs=moving, start=True, stop=True)
+                banks[(h, tb0)] = ps[:, :, 0:n * P].rearrange("p j c -> p c j")
 
         def scores_out(h, tb0, n, engine):
             if tb0 == 0:
                 gs[h] = g_pool.tile([P, PACK, P, PACK], BF16, name="g", align_bytes=64)
-            src = banks[(h, tb0)][:, :, 0:n * P].rearrange("p j c -> p c j")
+            src = banks[(h, tb0)]
             dst = gs[h][:, tb0:tb0 + n].rearrange("p b c j -> p (b c) j")
             if engine == VECTOR:
                 nc.vector.tensor_copy(out=dst, in_=src)

@@ -18,15 +18,18 @@ PAIR = 2
 HALF = 2
 SCALAR = 0
 VECTOR = 1
-WOVEN = ((4, 2), (9, 2), (15, 2), (15, 3),)
+WOVEN = ((5, 2), (9, 2), (15, 0))
 
 
 def units_of(h):
     if h == 0:
-        return ((0, 1, SCALAR), (1, 1, SCALAR), (2, 2, VECTOR))
+        return ((0, 1, SCALAR), (1, 1, SCALAR), (2, 2, SCALAR))
+    if h == 1:
+        return ((0, 2, VECTOR), (2, 2, SCALAR))
     if h == H - 1:
         return ((0, 2, SCALAR), (2, 1, SCALAR), (3, 1, VECTOR))
     return ((0, 2, SCALAR), (2, 2, VECTOR if h % 2 == 0 and h < H - 2 else SCALAR))
+
 
 SCALAR_PRODUCTS = (1, 3, 5, 7)
 WARM_PASSES = 12
@@ -107,7 +110,10 @@ def tile_linearattention_pa_kernel(tc, q_rot, v, out):
 
         def qt_out(h):
             qt = qt_pool.tile([P, PACK, P], BF16, name="qt")
-            nc.vector.tensor_copy(out=qt[:], in_=pts[h][:])
+            if h % 4 == 0:
+                nc.scalar.copy(out=qt[:], in_=pts[h][:])
+            else:
+                nc.vector.tensor_copy(out=qt[:], in_=pts[h][:])
             qts[h] = qt
 
         def v_regroup(h0):
@@ -231,6 +237,6 @@ def tile_linearattention_pa_kernel(tc, q_rot, v, out):
         quantise(H - 1, 2, 2)
         product(H - 1, 2, 2, True)
         product_out(H - 3, 0, PACK, True)
-        product_out(H - 2, 0, PACK, False)
+        product_out(H - 2, 0, PACK, True)
         product_out(H - 1, 0, 2, True)
-        product_out(H - 1, 2, 2, False)
+        product_out(H - 1, 2, 2, True)

@@ -18,7 +18,7 @@ PAIR = 2
 HALF = 2
 SCALAR = 0
 VECTOR = 1
-WOVEN = ((5, 2), (9, 2), (15, 0))
+WOVEN = ((7, 2), (13, 2), (14, 0), (15, 2))
 
 
 def units_of(h):
@@ -32,7 +32,7 @@ def units_of(h):
 
 
 SCALAR_PRODUCTS = (1, 3, 5, 7)
-WARM_PASSES = 12
+WARM_PASSES = 11
 
 
 def tile_linearattention_pa_kernel(tc, q_rot, v, out):

@@ -18,7 +18,6 @@ PAIR = 2
 HALF = 2
 SCALAR = 0
 VECTOR = 1
-WOVEN = ((7, 2), (13, 2), (14, 0), (15, 2))
 
 
 def units_of(h):
@@ -31,8 +30,14 @@ def units_of(h):
     return ((0, 2, SCALAR), (2, 2, VECTOR if h % 2 == 0 and h < H - 2 else SCALAR))
 
 
-SCALAR_PRODUCTS = (1, 3, 5, 7)
-WARM_PASSES = 11
+def is_woven(h, tb0):
+    if h == H - 1:
+        return tb0 == 2
+    return h % 3 == 2 and tb0 == (0 if h % 2 == 0 else 2)
+
+
+SCALAR_PRODUCTS = (1, 3, 5, 7, 9)
+WARM_PASSES = 3
 
 
 def tile_linearattention_pa_kernel(tc, q_rot, v, out):
@@ -53,7 +58,7 @@ def tile_linearattention_pa_kernel(tc, q_rot, v, out):
         psum_o = ctx.enter_context(tc.psum_pool(name="pso", bufs=2))
         ctx.enter_context(tc.manual_schedule())
 
-        warm = keep.tile([P, P], BF16, name="warm")
+        warm = keep.tile([P, P], F32, name="warm")
         nc.vector.memset(warm[:], 0.0)
         warm_out = psum_o.tile([P, PACK, D], F32, name="po")
         for k in range(WARM_PASSES):
@@ -139,7 +144,7 @@ def tile_linearattention_pa_kernel(tc, q_rot, v, out):
         def scores(h, tb0, n):
             qt = qts[h]
             moving = qt[:, tb0:tb0 + n, :].rearrange("p b c -> p (b c)")
-            if (h, tb0) in WOVEN:
+            if is_woven(h, tb0):
                 ps = psum_s.tile([P, HALF * P, PACK], BF16, name="ps")
                 twice = moving.unsqueeze(2).to_broadcast([P, n * P, 2])
                 for j in (0, 2):

@@ -218,15 +218,17 @@ def tile_linearattention_pa_kernel(tc, q_rot, v, out):
             first = (len(units) + 1) // 2
             for k, (tb0, n, engine) in enumerate(units):
                 scores(i, tb0, n)
-                if k == first - 1 and i + 2 < H:
-                    transposes(i + 2)
-            if i >= 2:
+                if k == first - 1 and 3 <= i < H - 1:
+                    product(i - 3, 0, PACK, False)
+            if i + 2 < H:
+                transposes(i + 2)
+            else:
                 product(i - 2, 0, PACK, False)
             for tb0, n, engine in units[:first]:
                 scores_out(i, tb0, n, engine)
-            if i >= 3:
+            if i >= 3 and i % 2 == 1:
                 product_out(i - 3, 0, PACK, (i - 3) in SCALAR_PRODUCTS)
-            if i + 2 < H:
+            if i + 2 < H and (i == 0 or i % 2 == 1):
                 qt_out(i + 2)
             if i >= 1:
                 quantise(i - 1, 0, PACK)
@@ -234,8 +236,12 @@ def tile_linearattention_pa_kernel(tc, q_rot, v, out):
                 v_quantise(i)
                 if i + PAIR < H:
                     v_regroup(i + PAIR)
+            if 0 < i < H - 2 and i % 2 == 0:
+                qt_out(i + 2)
             for tb0, n, engine in units[first:]:
                 scores_out(i, tb0, n, engine)
+            if i >= 3 and i % 2 == 0:
+                product_out(i - 3, 0, PACK, (i - 3) in SCALAR_PRODUCTS)
         quantise(H - 1, 0, 2)
         product(H - 2, 0, PACK, False)
         product(H - 1, 0, 2, True)

@@ -81,7 +81,10 @@ def tile_linearattention_pa_kernel(tc, q_rot, v, out):
             nc.sync.dma_start(out=vs_[:], in_=vv[:, h0:h0 + PAIR])
             v_pair[h0] = vs_
 
-        load_q(0, 1)
+        qs0 = keep.tile([P, 1, PACK, D], BF16, name="q0")
+        nc.sync.dma_start(out=qs0[:, :, 0:2], in_=qv[:, 0:1, 0:2])
+        nc.sync.dma_start(out=qs0[:, :, 2:4], in_=qv[:, 0:1, 2:4])
+        q_head[0] = qs0[:, 0]
         load_q(1, 1)
         load_v(0)
         load_q(2, 2)
@@ -109,13 +112,19 @@ def tile_linearattention_pa_kernel(tc, q_rot, v, out):
 
         def transposes(h):
             pt = psum_t.tile([P, PACK, P], BF16, name="pt")
-            for j in range(PACK):
-                nc.tensor.transpose(pt[:, j, :], q_head[h][:, j, :], ident[:])
             pts[h] = pt
+            for j in range(PACK):
+                if h == 0 and j == 2:
+                    pt = psum_o.tile([P, PACK, P], BF16, name="po")
+                    pts[-1] = pt
+                nc.tensor.transpose(pt[:, j, :], q_head[h][:, j, :], ident[:])
 
         def qt_out(h):
             qt = qt_pool.tile([P, PACK, P], BF16, name="qt")
-            if h % 4 == 0:
+            if h == 0:
+                nc.scalar.copy(out=qt[:, 0:2], in_=pts[0][:, 0:2])
+                nc.vector.tensor_copy(out=qt[:, 2:4], in_=pts[-1][:, 2:4])
+            elif h % 4 == 0:
                 nc.scalar.copy(out=qt[:], in_=pts[h][:])
             else:
                 nc.vector.tensor_copy(out=qt[:], in_=pts[h][:])

@@ -33,7 +33,9 @@ def units_of(h):
 def is_woven(h, tb0):
     if h == H - 1:
         return tb0 == 2
-    return h % 3 == 2 and tb0 == (0 if h % 2 == 0 else 2)
+    if h == 10:
+        return tb0 == 2
+    return h > 2 and h % 3 == 2 and tb0 == (0 if h % 2 == 0 else 2)
 
 
 SCALAR_PRODUCTS = (1, 3, 5, 7, 9)
@@ -87,7 +89,8 @@ def tile_linearattention_pa_kernel(tc, q_rot, v, out):
         q_head[0] = qs0[:, 0]
         load_q(1, 1)
         load_v(0)
-        load_q(2, 2)
+        load_q(2, 1)
+        load_q(3, 1)
         load_v(2)
         load_q(4, 4)
         load_v(4)
@@ -131,7 +134,10 @@ def tile_linearattention_pa_kernel(tc, q_rot, v, out):
             qts[h] = qt
 
         def v_regroup(h0):
-            vg = vg_pool.tile([P, PAIR, D, PACK], BF16, name="vg", align_bytes=64)
+            if h0 == 0:
+                vg = keep.tile([P, PAIR, D, PACK], BF16, name="vg0", align_bytes=64)
+            else:
+                vg = vg_pool.tile([P, PAIR, D, PACK], BF16, name="vg", align_bytes=64)
             nc.gpsimd.tensor_scalar(
                 out=vg[:],
                 in0=v_pair[h0][:].rearrange("p h j d -> p h d j"),
@@ -220,6 +226,7 @@ def tile_linearattention_pa_kernel(tc, q_rot, v, out):
         transposes(0)
         qt_out(0)
         v_regroup(0)
+        v_regroup(PAIR)
         transposes(1)
         qt_out(1)
         for i in range(H):
@@ -237,11 +244,13 @@ def tile_linearattention_pa_kernel(tc, q_rot, v, out):
                 scores_out(i, tb0, n, engine)
             if i >= 3 and i % 2 == 1:
                 product_out(i - 3, 0, PACK, (i - 3) in SCALAR_PRODUCTS)
+            if i == 1:
+                v_quantise(0)
             if i + 2 < H and (i == 0 or i % 2 == 1):
                 qt_out(i + 2)
             if i >= 1:
                 quantise(i - 1, 0, PACK)
-            if i % PAIR == 0:
+            if i % PAIR == 0 and i > 0:
                 v_quantise(i)
                 if i + PAIR < H:
                     v_regroup(i + PAIR)

from contextlib import ExitStack

import concourse.mybir as mybir
from concourse.masks import make_identity

BF16 = mybir.dt.bfloat16
F32 = mybir.dt.float32
U32 = mybir.dt.uint32
U8 = mybir.dt.uint8
FP8X4 = mybir.dt.float8_e4m3fn_x4

P = 128
PACK = 4
H, T, D = 16, 512, 128
FLOPS = 2 * 2 * H * T * T * D

PAIR = 2
HALF = 2
SCALAR = 0
VECTOR = 1


def units_of(h):
    if h == 0:
        return ((0, 1, SCALAR), (1, 1, SCALAR), (2, 2, SCALAR))
    if h == 1:
        return ((0, 2, VECTOR), (2, 2, SCALAR))
    if h == H - 1:
        return ((0, 2, SCALAR), (2, 1, SCALAR), (3, 1, VECTOR))
    return ((0, 2, SCALAR), (2, 2, VECTOR if h % 2 == 0 and h < H - 2 else SCALAR))


def is_woven(h, tb0):
    if h == H - 1:
        return tb0 == 2
    if h == 10:
        return tb0 == 2
    return h > 2 and h % 3 == 2 and tb0 == (0 if h % 2 == 0 else 2)


SCALAR_PRODUCTS = (1, 3, 5, 7, 9)
WARM_PASSES = 3


def tile_linearattention_pa_kernel(tc, q_rot, v, out):
    nc = tc.nc
    qv = q_rot.rearrange("b h (p j) d -> p (b h) j d", j=PACK)
    vv = v.rearrange("b h (p j) d -> p (b h) j d", j=PACK)
    ov = out.rearrange("b h (p j) d -> p (b h) j d", j=PACK)

    with ExitStack() as ctx:
        keep = ctx.enter_context(tc.tile_pool(name="keep", bufs=1))
        qt_pool = ctx.enter_context(tc.tile_pool(name="qtp", bufs=16))
        g_pool = ctx.enter_context(tc.tile_pool(name="gp", bufs=16))
        c_pool = ctx.enter_context(tc.tile_pool(name="cp", bufs=16))
        vg_pool = ctx.enter_context(tc.tile_pool(name="vgp", bufs=1))
        o_pool = ctx.enter_context(tc.tile_pool(name="op", bufs=16))
        psum_t = ctx.enter_context(tc.psum_pool(name="pst", bufs=2))
        psum_s = ctx.enter_context(tc.psum_pool(name="pss", bufs=4))
        psum_o = ctx.enter_context(tc.psum_pool(name="pso", bufs=2))
        ctx.enter_context(tc.manual_schedule())

        warm = keep.tile([P, P], F32, name="warm")
        nc.vector.memset(warm[:], 0.0)
        warm_out = psum_o.tile([P, PACK, D], F32, name="po")
        for k in range(WARM_PASSES):
            nc.tensor.matmul(warm_out[:, k % PACK, :], lhsT=warm[:], rhs=warm[:], start=True, stop=True)

        ident = keep.tile([P, P], BF16, name="ident")
        make_identity(nc, ident[:])

        q_head = {}
        v_pair = {}

        def load_q(h0, n):
            qs = keep.tile([P, n, PACK, D], BF16, name="q%d" % h0)
            nc.sync.dma_start(out=qs[:], in_=qv[:, h0:h0 + n])
            for k in range(n):
                q_head[h0 + k] = qs[:, k]

        def load_v(h0):
            vs_ = keep.tile([P, PAIR, PACK, D], BF16, name="v%d" % h0)
            nc.sync.dma_start(out=vs_[:], in_=vv[:, h0:h0 + PAIR])
            v_pair[h0] = vs_

        qs0 = keep.tile([P, 1, PACK, D], BF16, name="q0")
        nc.sync.dma_start(out=qs0[:, :, 0:2], in_=qv[:, 0:1, 0:2])
        nc.sync.dma_start(out=qs0[:, :, 2:4], in_=qv[:, 0:1, 2:4])
        q_head[0] = qs0[:, 0]
        load_q(1, 1)
        load_v(0)
        load_q(2, 1)
        load_q(3, 1)
        load_v(2)
        load_q(4, 4)
        load_v(4)
        load_v(6)
        load_q(8, 4)
        load_v(8)
        load_v(10)
        load_q(12, 4)
        load_v(12)
        load_v(14)

        v_codes = keep.tile([P, H * D], U32, name="v_codes", align_bytes=64)
        v_scales = keep.tile([P, H * D], U8, name="v_scales", align_bytes=64)

        pts = {}
        qts = {}
        banks = {}
        gs = {}
        codes = {}
        vgs = {}
        pos = {}

        def transposes(h):
            pt = psum_t.tile([P, PACK, P], BF16, name="pt")
            pts[h] = pt
            for j in range(PACK):
                if h == 0 and j == 2:
                    pt = psum_o.tile([P, PACK, P], BF16, name="po")
                    pts[-1] = pt
                nc.tensor.transpose(pt[:, j, :], q_head[h][:, j, :], ident[:])

        def qt_out(h):
            qt = qt_pool.tile([P, PACK, P], BF16, name="qt")
            if h == 0:
                nc.scalar.copy(out=qt[:, 0:2], in_=pts[0][:, 0:2])
                nc.vector.tensor_copy(out=qt[:, 2:4], in_=pts[-1][:, 2:4])
            elif h % 4 == 0:
                nc.scalar.copy(out=qt[:], in_=pts[h][:])
            else:
                nc.vector.tensor_copy(out=qt[:], in_=pts[h][:])
            qts[h] = qt

        def v_regroup(h0):
            if h0 == 0:
                vg = keep.tile([P, PAIR, D, PACK], BF16, name="vg0", align_bytes=64)
            else:
                vg = vg_pool.tile([P, PAIR, D, PACK], BF16, name="vg", align_bytes=64)
            nc.gpsimd.tensor_scalar(
                out=vg[:],
                in0=v_pair[h0][:].rearrange("p h j d -> p h d j"),
                scalar1=1.0,
                scalar2=0.0,
                op0=mybir.AluOpType.mult,
                op1=mybir.AluOpType.add,
            )
            vgs[h0] = vg

        def v_quantise(h0):
            cols = slice(h0 * D, (h0 + PAIR) * D)
            nc.vector.quantize_mx(
                out=v_codes[:, cols].bitcast(FP8X4),
                scales=v_scales[:, cols],
                in_=vgs[h0][:].rearrange("p h d j -> p (h d j)"),
            )

        def scores(h, tb0, n):
            qt = qts[h]
            moving = qt[:, tb0:tb0 + n, :].rearrange("p b c -> p (b c)")
            if is_woven(h, tb0):
                ps = psum_s.tile([P, HALF * P, PACK], BF16, name="ps")
                twice = moving.unsqueeze(2).to_broadcast([P, n * P, 2])
                for j in (0, 2):
                    nc.tensor.matmul(ps[:, 0:n * P, j:j + 2], lhsT=qt[:, j + 1, :], rhs=twice, start=True, stop=True)
                    nc.tensor.matmul(ps[:, 0:n * P, j], lhsT=qt[:, j, :], rhs=moving, start=True, stop=True)
                banks[(h, tb0)] = ps[:, 0:n * P, :]
            else:
                ps = psum_s.tile([P, PACK, HALF * P], BF16, name="ps")
                for j in range(PACK):
                    nc.tensor.matmul(ps[:, j, 0:n * P], lhsT=qt[:, j, :], rhs=moving, start=True, stop=True)
                banks[(h, tb0)] = ps[:, :, 0:n * P].rearrange("p j c -> p c j")

        def scores_out(h, tb0, n, engine):
            if tb0 == 0:
                gs[h] = g_pool.tile([P, PACK, P, PACK], BF16, name="g", align_bytes=64)
            src = banks[(h, tb0)]
            dst = gs[h][:, tb0:tb0 + n].rearrange("p b c j -> p (b c) j")
            if engine == VECTOR:
                nc.vector.tensor_copy(out=dst, in_=src)
            else:
                nc.scalar.copy(out=dst, in_=src)

        def quantise(h, tb0, n):
            if tb0 == 0:
                sc_new = c_pool.tile([P, T], U32, name="sc", align_bytes=64)
                ss_new = c_pool.tile([P, T], U8, name="ss", align_bytes=64)
                codes[h] = (sc_new, ss_new)
            sc, ss = codes[h]
            cols = slice(tb0 * P, (tb0 + n) * P)
            nc.vector.quantize_mx(
                out=sc[:, cols].bitcast(FP8X4),
                scales=ss[:, cols],
                in_=gs[h][:, tb0:tb0 + n].rearrange("p b c j -> p (b c j)"),
            )

        def product(h, tb0, n, in_score_bank):
            sc, ss = codes[h]
            if in_score_bank:
                po = psum_s.tile([P, PACK, D], F32, name="ps")
            else:
                po = psum_o.tile([P, PACK, D], F32, name="po")
            vcols = slice(h * D, (h + 1) * D)
            for k in range(n):
                cols = slice((tb0 + k) * P, (tb0 + k + 1) * P)
                nc.tensor.matmul_mx(
                    out=po[:, k, :],
                    lhsT=sc[:, cols].bitcast(FP8X4),
                    lhsT_scale=ss[:, cols],
                    rhs=v_codes[:, vcols].bitcast(FP8X4),
                    rhs_scale=v_scales[:, vcols],
                    start=True,
                    stop=True,
                )
            pos[(h, tb0)] = po

        def product_out(h, tb0, n, on_scalar):
            o_sb = o_pool.tile([P, PACK, D], F32, name="o_sb")
            if on_scalar:
                nc.scalar.copy(out=o_sb[:, 0:n, :], in_=pos[(h, tb0)][:, 0:n, :])
            else:
                nc.vector.tensor_copy(out=o_sb[:, 0:n, :], in_=pos[(h, tb0)][:, 0:n, :])
            nc.sync.dma_start(out=ov[:, h, tb0:tb0 + n], in_=o_sb[:, 0:n, :])

        transposes(0)
        qt_out(0)
        v_regroup(0)
        v_regroup(PAIR)
        transposes(1)
        qt_out(1)
        for i in range(H):
            units = units_of(i)
            first = (len(units) + 1) // 2
            for k, (tb0, n, engine) in enumerate(units):
                scores(i, tb0, n)
                if k == first - 1 and 3 <= i < H - 1:
                    product(i - 3, 0, PACK, False)
            if i + 2 < H:
                transposes(i + 2)
            else:
                product(i - 2, 0, PACK, False)
            for tb0, n, engine in units[:first]:
                scores_out(i, tb0, n, engine)
            if i >= 3 and i % 2 == 1:
                product_out(i - 3, 0, PACK, (i - 3) in SCALAR_PRODUCTS)
            if i == 1:
                v_quantise(0)
            if i + 2 < H and (i == 0 or i % 2 == 1):
                qt_out(i + 2)
            if i >= 1:
                quantise(i - 1, 0, PACK)
            if i % PAIR == 0 and i > 0:
                v_quantise(i)
                if i + PAIR < H:
                    v_regroup(i + PAIR)
            if 0 < i < H - 2 and i % 2 == 0:
                qt_out(i + 2)
            for tb0, n, engine in units[first:]:
                scores_out(i, tb0, n, engine)
            if i >= 3 and i % 2 == 0:
                product_out(i - 3, 0, PACK, (i - 3) in SCALAR_PRODUCTS)
        quantise(H - 1, 0, 2)
        product(H - 2, 0, PACK, False)
        product(H - 1, 0, 2, True)
        quantise(H - 1, 2, 2)
        product(H - 1, 2, 2, True)
        product_out(H - 3, 0, PACK, True)
        product_out(H - 2, 0, PACK, True)
        product_out(H - 1, 0, 2, True)
        product_out(H - 1, 2, 2, True)
